import numpy as np
import ml_dtypes


def mxq(x, axis, fmt="e4m3"):
    dtype, down = {"e4m3": (ml_dtypes.float8_e4m3fn, 7), "e5m2": (ml_dtypes.float8_e5m2, 14)}[fmt]
    v = np.moveaxis(np.asarray(x, np.float32).astype(ml_dtypes.bfloat16).astype(np.float64), axis, -1)
    blocks = v.reshape(v.shape[:-1] + (-1, 32))
    amax = np.abs(blocks).max(-1, keepdims=True)
    byte = np.maximum(np.where(amax > 0, np.frexp(amax)[1] - 1 + 127, 0) - down, 1)
    scale = np.exp2(byte - 127.0)
    codes = (blocks / scale).astype(np.float32).astype(dtype).astype(np.float64)
    return np.moveaxis((codes * scale).reshape(v.shape), -1, axis)


WIDE = False


def mx_kscale(k):
    if not WIDE:
        return np.ones(k)
    levels = np.array([10, -10, 5, -5, 0])
    a = np.random.permutation(np.resize(levels, k // 512 * 4)).reshape(k // 512, 4)
    idx = np.arange(k)
    return np.exp2(a[idx // 512, idx % 128 // 32])


BF16 = ml_dtypes.bfloat16


def bf(x):
    return np.asarray(x, np.float32).astype(BF16)


def f64(x):
    return np.asarray(x).astype(np.float64)


E2M1 = np.array([0.0, 0.5, 1.0, 1.5, 2.0, 3.0, 4.0, 6.0, -0.0, -0.5, -1.0, -1.5, -2.0, -3.0, -4.0, -6.0])


def pack_weight(w, fmt):
    k, n = w.shape
    w = f64(bf(w)).reshape(k // 32, 32, n)
    amax = np.abs(w).max(1)
    if fmt == "e4m3":
        byte = np.frexp(amax)[1] - 1 + 127 - 7
    else:
        mant, ex = np.frexp(amax / 6.0)
        byte = np.where(mant > 0.5, ex, ex - 1) + 127
    byte = np.clip(np.where(amax > 0, byte, 1), 1, 254)
    scaled = (w * np.exp2(127.0 - byte)[:, None, :]).reshape(k, n).astype(np.float32)
    by_word = np.ascontiguousarray(scaled.reshape(k // 512, 128, 4, n).transpose(0, 1, 3, 2))
    if fmt == "e4m3":
        words = by_word.astype(ml_dtypes.float8_e4m3fn).view(np.uint8)
    else:
        c = by_word.astype(ml_dtypes.float4_e2m1fn).view(np.uint8) & 0xF
        words = c[..., 0::2] | (c[..., 1::2] << 4)
    return np.ascontiguousarray(words), np.ascontiguousarray(byte.astype(np.uint8).reshape(k // 512, 16, n))


def unpack_weight(words, scales, fmt):
    g, p, n, _ = words.shape
    if fmt == "e4m3":
        vals = np.ascontiguousarray(words).view(ml_dtypes.float8_e4m3fn).astype(np.float64)
    else:
        nib = np.empty((g, p, n, 4), np.uint8)
        nib[..., 0::2] = words & 0xF
        nib[..., 1::2] = words >> 4
        vals = E2M1[nib]
    vals = vals * np.repeat(np.exp2(scales.astype(np.float64) - 127.0), 8, axis=1)[..., None]
    return vals.transpose(0, 1, 3, 2).reshape(g * 512, n)


B, T, DIM, H, D = 16, 1024, 128, 4, 128
E = H * D


def softmax(z):
    e = np.exp(z - z.max(-1, keepdims=True))
    return e / e.sum(-1, keepdims=True)


def setup_inputs():
    u = mx_kscale(E).reshape(H, D)
    q = softmax(3.0 * np.random.standard_normal((B, H, T, D)))
    k_sum = (T / D) * np.exp(0.3 * np.random.standard_normal((B, H, 1, D)))
    amp = 2.0 * np.sqrt(T * np.mean(q * q))
    context = k_sum.transpose(0, 1, 3, 2) * 0.2 * np.random.standard_normal((1, H, 1, D)) + amp * np.random.standard_normal((B, H, D, D))
    Wp = np.random.standard_normal((DIM, E)) * 2.0 / np.sqrt(E) / u.reshape(E)
    words, scales = pack_weight(Wp.T, "e4m3")
    return {"q": bf(q * u[None, :, None, :]),
            "k_sum": bf(k_sum / u[None, :, None, :]),
            "context": bf(context * u[None, :, None, :] / u[None, :, :, None]),
            "Wp_words": words,
            "Wp_scales": scales,
            "bp": bf(np.random.standard_normal(DIM) * 0.2)}


def reference(q, k_sum, context, Wp_words, Wp_scales, bp):
    d_inv = 1.0 / (f64(q) * f64(k_sum)).sum(axis=-1, keepdims=True)
    o = (f64(q) @ f64(context)) * d_inv + f64(q)
    o = o.transpose(0, 2, 1, 3).reshape(B, T, E)
    return (mxq(o, 2, "e4m3") @ unpack_weight(Wp_words, Wp_scales, "e4m3")) + f64(bp)

@@ -1,0 +1,201 @@
+from contextlib import ExitStack
+
+import concourse.mybir as mybir
+from concourse.masks import make_identity
+
+BF16 = mybir.dt.bfloat16
+F32 = mybir.dt.float32
+I32 = mybir.dt.int32
+U8 = mybir.dt.uint8
+U32 = mybir.dt.uint32
+FP8X4 = mybir.dt.float8_e4m3fn_x4
+MULT = mybir.AluOpType.mult
+ADD = mybir.AluOpType.add
+
+P = 128
+B, H, T, D = 16, 4, 1024, 128
+E = H * D
+DIM = 128
+PACK = 4
+
+TILES = T // P
+PAIR = 2
+PAIR_UNITS = PAIR * H
+QUAD = 4
+PAIRS = B * TILES // PAIR
+PAIRS_IN_BATCH = TILES // PAIR
+PAIRS_IN_QUAD = QUAD // PAIR
+BANK_UNITS = 3
+CTX_PITCH = 144
+AHEAD = 3
+
+FLOPS = 2 * B * H * T * D * D + 2 * B * T * E * DIM
+
+
+def tile_linearattention_pb_t_kernel(tc, q, k_sum, context, Wp_words, Wp_scales, bp, out):
+    nc = tc.nc
+    with ExitStack() as stack:
+        const = stack.enter_context(tc.tile_pool(name="const", bufs=1))
+        batch_pool = stack.enter_context(tc.tile_pool(name="batch", bufs=AHEAD + 2))
+        work = stack.enter_context(tc.tile_pool(name="work", bufs=3))
+        psum_qt = stack.enter_context(tc.psum_pool(name="psum_qt", bufs=2))
+        psum_o = stack.enter_context(tc.psum_pool(name="psum_o", bufs=3))
+        psum_omt = stack.enter_context(tc.psum_pool(name="psum_omt", bufs=2))
+        psum_out = stack.enter_context(tc.psum_pool(name="psum_out", bufs=1))
+
+        ident_bf16 = const.tile([P, P], BF16)
+        make_identity(nc, ident_bf16[:])
+        ident_f32 = const.tile([P, P], F32)
+        make_identity(nc, ident_f32[:])
+
+        ksum_rows = const.tile([P, D], BF16)
+        nc.vector.memset(ksum_rows[:], 0.0)
+        nc.sync.dma_start(out=ksum_rows[0 : B * H, :], in_=k_sum.rearrange("b h o d -> (b h o) d"))
+        ksum_ps = psum_qt.tile([P, PAIR_UNITS, P], BF16, tag="qt_ps")
+        nc.tensor.transpose(ksum_ps[:, 0, :], ksum_rows[:], ident_bf16[:])
+        ksum_cols = const.tile([P, B * H], BF16)
+        nc.vector.tensor_copy(out=ksum_cols[:], in_=ksum_ps[:, 0, 0 : B * H])
+
+        q_of = {}
+        ctx_of = {}
+        qt_of = {}
+        om_of = {}
+        grouped_of = {}
+        codes_of = {}
+
+        def load_batch(b):
+            ctx_sb = batch_pool.tile([P, H, CTX_PITCH], BF16)
+            nc.sync.dma_start(out=ctx_sb[:, :, 0:D], in_=context[b].rearrange("h d e -> d h e"))
+            nc.gpsimd.tensor_copy(
+                out=ctx_sb[:, :, D : D + 1], in_=ksum_cols[:, H * b : H * (b + 1)].unsqueeze(2)
+            )
+            q_sb = batch_pool.tile([P, H, TILES, D], BF16)
+            nc.sync.dma_start(
+                out=q_sb[:].rearrange("p h a d -> p h (a d)"),
+                in_=q[b].rearrange("h (p a) d -> p h (a d)", a=TILES),
+            )
+            ctx_of[b] = ctx_sb
+            q_of[b] = q_sb
+
+        def where(pair):
+            return pair // PAIRS_IN_BATCH, PAIR * (pair % PAIRS_IN_BATCH)
+
+        def transpose_q(pair):
+            b, a0 = where(pair)
+            qt_ps = psum_qt.tile([P, PAIR_UNITS, P], BF16, tag="qt_ps")
+            for unit in range(PAIR_UNITS):
+                nc.tensor.transpose(qt_ps[:, unit, :], q_of[b][:, unit % H, a0 + unit // H, :], ident_bf16[:])
+            qt_sb = work.tile([P, PAIR_UNITS, P], BF16)
+            nc.scalar.copy(out=qt_sb[:], in_=qt_ps[:])
+            qt_of[pair] = qt_sb
+
+        def attend(pair):
+            b, a0 = where(pair)
+            om_sb = work.tile([P, PAIR, E], BF16)
+            for first in range(0, PAIR_UNITS, BANK_UNITS):
+                units = list(range(first, min(first + BANK_UNITS, PAIR_UNITS)))
+                o_ps = psum_o.tile([P, BANK_UNITS, D + 1], F32)
+                for slot, unit in enumerate(units):
+                    nc.tensor.matmul(
+                        o_ps[:, slot, :],
+                        lhsT=qt_of[pair][:, unit, :],
+                        rhs=ctx_of[b][:, unit % H, 0 : D + 1],
+                        start=True,
+                        stop=True,
+                    )
+                d_inv = work.tile([P, BANK_UNITS], F32)
+                nc.vector.reciprocal(out=d_inv[:, 0 : len(units)], in_=o_ps[:, 0 : len(units), D])
+                for slot, unit in enumerate(units):
+                    h = unit % H
+                    nc.vector.scalar_tensor_tensor(
+                        out=om_sb[:, unit // H, D * h : D * (h + 1)],
+                        in0=o_ps[:, slot, 0:D],
+                        scalar=d_inv[:, slot : slot + 1],
+                        in1=q_of[b][:, h, a0 + unit // H, :],
+                        op0=MULT,
+                        op1=ADD,
+                    )
+            om_of[pair] = om_sb
+
+        def transpose_om(pair):
+            quad, half = pair // PAIRS_IN_QUAD, pair % PAIRS_IN_QUAD
+            if half == 0:
+                grouped = work.tile([P, QUAD * P * PACK], BF16, align_bytes=64)
+                grouped_of[quad] = grouped
+            omt_ps = psum_omt.tile([P, PAIR, 2, P], F32)
+            for tile_in_pair in range(PAIR):
+                om_words = om_of[pair][:, tile_in_pair, :].bitcast(F32)
+                for u in range(2):
+                    nc.tensor.transpose(omt_ps[:, tile_in_pair, u, :], om_words[:, u : E // 2 : 2], ident_f32[:])
+            words = PAIR * P * 2
+            nc.scalar.copy(
+                out=grouped_of[quad][:]
+                .bitcast(F32)[:, words * half : words * (half + 1)]
+                .rearrange("p (i t u) -> p i t u", i=PAIR, u=2),
+                in_=omt_ps[:].rearrange("p i u t -> p i t u"),
+            )
+
+        def quantise(quad):
+            codes = work.tile([P, QUAD * P], U32, align_bytes=64)
+            scales = work.tile([P, QUAD * P], U8, align_bytes=64)
+            nc.vector.quantize_mx(out=codes[:].bitcast(FP8X4), scales=scales[:], in_=grouped_of[quad][:])
+            codes_of[quad] = (codes, scales)
+
+        def project(quad):
+            codes, scales = codes_of[quad]
+            out_ps = psum_out.tile([P, QUAD, DIM], F32)
+            for i in range(QUAD):
+                nc.tensor.matmul_mx(
+                    out=out_ps[:, i, :],
+                    lhsT=codes[:, P * i : P * (i + 1)].bitcast(FP8X4),
+                    lhsT_scale=scales[:, P * i : P * (i + 1)],
+                    rhs=w_codes[:].bitcast(FP8X4),
+                    rhs_scale=w_scales[:],
+                    start=True,
+                    stop=True,
+                )
+            no_bias = work.tile([P, QUAD, DIM], F32)
+            nc.scalar.copy(out=no_bias[:], in_=out_ps[:])
+            result = work.tile([P, QUAD, DIM], F32)
+            nc.gpsimd.tensor_tensor(
+                out=result[:], in0=no_bias[:], in1=bias[:].unsqueeze(1).to_broadcast([P, QUAD, DIM]), op=ADD
+            )
+            b, a0 = where(quad * PAIRS_IN_QUAD)
+            nc.sync.dma_start(
+                out=out[b].rearrange("(p a) n -> p a n", a=TILES)[:, a0 : a0 + QUAD, :], in_=result[:]
+            )
+
+        load_batch(0)
+
+        w_codes = const.tile([P, PACK * DIM], U8, align_bytes=64)
+        nc.sync.dma_start(
+            out=w_codes[:].bitcast(I32), in_=Wp_words[0].rearrange("p n j -> p (n j)").bitcast(I32)
+        )
+        w_scales = const.tile([P, DIM], U8, align_bytes=64)
+        nc.vector.memset(w_scales[:].bitcast(I32), 0)
+        for quadrant in range(4):
+            nc.sync.dma_start(
+                out=w_scales[32 * quadrant : 32 * quadrant + 4, :].bitcast(I32),
+                in_=Wp_scales[0, 4 * quadrant : 4 * quadrant + 4, :].bitcast(I32),
+            )
+
+        bias_bf16 = const.tile([P, DIM], BF16)
+        nc.sync.dma_start(out=bias_bf16[:], in_=bp.partition_broadcast(P))
+        bias = const.tile([P, DIM], F32)
+        nc.vector.tensor_copy(out=bias[:], in_=bias_bf16[:])
+
+        for b in range(1, AHEAD):
+            load_batch(b)
+        for step in range(PAIRS + 4):
+            if step % PAIRS_IN_BATCH == 0 and step // PAIRS_IN_BATCH + AHEAD < B:
+                load_batch(step // PAIRS_IN_BATCH + AHEAD)
+            if step < PAIRS:
+                transpose_q(step)
+            if 0 <= step - 1 < PAIRS:
+                attend(step - 1)
+            if 0 <= step - 2 < PAIRS:
+                transpose_om(step - 2)
+            if 0 <= step - 3 < PAIRS and (step - 3) % PAIRS_IN_QUAD == PAIRS_IN_QUAD - 1:
+                quantise((step - 3) // PAIRS_IN_QUAD)
+            if 0 <= step - 4 < PAIRS and (step - 4) % PAIRS_IN_QUAD == PAIRS_IN_QUAD - 1:
+                project((step - 4) // PAIRS_IN_QUAD)

@@ -26,6 +26,7 @@ PAIRS = B * TILES // PAIR
 PAIRS_IN_BATCH = TILES // PAIR
 PAIRS_IN_QUAD = QUAD // PAIR
 BANK_UNITS = 3
+PAIR_BANKS = 3
 CTX_PITCH = 144
 AHEAD = 3
 
@@ -35,13 +36,15 @@ FLOPS = 2 * B * H * T * D * D + 2 * B * T * E * DIM
 def tile_linearattention_pb_t_kernel(tc, q, k_sum, context, Wp_words, Wp_scales, bp, out):
     nc = tc.nc
     with ExitStack() as stack:
+        stack.enter_context(tc.manual_schedule())
         const = stack.enter_context(tc.tile_pool(name="const", bufs=1))
         batch_pool = stack.enter_context(tc.tile_pool(name="batch", bufs=AHEAD + 2))
-        work = stack.enter_context(tc.tile_pool(name="work", bufs=3))
-        psum_qt = stack.enter_context(tc.psum_pool(name="psum_qt", bufs=2))
-        psum_o = stack.enter_context(tc.psum_pool(name="psum_o", bufs=3))
-        psum_omt = stack.enter_context(tc.psum_pool(name="psum_omt", bufs=2))
-        psum_out = stack.enter_context(tc.psum_pool(name="psum_out", bufs=1))
+        work = stack.enter_context(tc.tile_pool(name="work", bufs=4))
+        to_vector = stack.enter_context(tc.psum_pool(name="to_vector", bufs=4))
+        to_scalar = stack.enter_context(tc.psum_pool(name="to_scalar", bufs=4))
+
+        w_scales = const.tile([P, DIM], U8, align_bytes=64)
+        nc.vector.memset(w_scales[:].bitcast(I32), 0)
 
         ident_bf16 = const.tile([P, P], BF16)
         make_identity(nc, ident_bf16[:])
@@ -51,14 +54,15 @@ def tile_linearattention_pb_t_kernel(tc, q, k_sum, context, Wp_words, Wp_scales,
         ksum_rows = const.tile([P, D], BF16)
         nc.vector.memset(ksum_rows[:], 0.0)
         nc.sync.dma_start(out=ksum_rows[0 : B * H, :], in_=k_sum.rearrange("b h o d -> (b h o) d"))
-        ksum_ps = psum_qt.tile([P, PAIR_UNITS, P], BF16, tag="qt_ps")
+        ksum_ps = to_scalar.tile([P, PAIR_UNITS, P], BF16, tag="to_scalar")
         nc.tensor.transpose(ksum_ps[:, 0, :], ksum_rows[:], ident_bf16[:])
         ksum_cols = const.tile([P, B * H], BF16)
-        nc.vector.tensor_copy(out=ksum_cols[:], in_=ksum_ps[:, 0, 0 : B * H])
+        nc.scalar.copy(out=ksum_cols[:], in_=ksum_ps[:, 0, 0 : B * H])
 
         q_of = {}
         ctx_of = {}
         qt_of = {}
+        product_of = {}
         om_of = {}
         grouped_of = {}
         codes_of = {}
@@ -80,49 +84,59 @@ def tile_linearattention_pb_t_kernel(tc, q, k_sum, context, Wp_words, Wp_scales,
         def where(pair):
             return pair // PAIRS_IN_BATCH, PAIR * (pair % PAIRS_IN_BATCH)
 
+        def units_of(bank):
+            first = BANK_UNITS * (bank % PAIR_BANKS)
+            return bank // PAIR_BANKS, list(range(first, min(first + BANK_UNITS, PAIR_UNITS)))
+
         def transpose_q(pair):
             b, a0 = where(pair)
-            qt_ps = psum_qt.tile([P, PAIR_UNITS, P], BF16, tag="qt_ps")
+            qt_ps = to_scalar.tile([P, PAIR_UNITS, P], BF16, tag="to_scalar")
             for unit in range(PAIR_UNITS):
                 nc.tensor.transpose(qt_ps[:, unit, :], q_of[b][:, unit % H, a0 + unit // H, :], ident_bf16[:])
             qt_sb = work.tile([P, PAIR_UNITS, P], BF16)
             nc.scalar.copy(out=qt_sb[:], in_=qt_ps[:])
             qt_of[pair] = qt_sb
 
-        def attend(pair):
+        def multiply(bank):
+            pair, units = units_of(bank)
             b, a0 = where(pair)
-            om_sb = work.tile([P, PAIR, E], BF16)
-            for first in range(0, PAIR_UNITS, BANK_UNITS):
-                units = list(range(first, min(first + BANK_UNITS, PAIR_UNITS)))
-                o_ps = psum_o.tile([P, BANK_UNITS, D + 1], F32)
-                for slot, unit in enumerate(units):
-                    nc.tensor.matmul(
-                        o_ps[:, slot, :],
-                        lhsT=qt_of[pair][:, unit, :],
-                        rhs=ctx_of[b][:, unit % H, 0 : D + 1],
-                        start=True,
-                        stop=True,
-                    )
-                d_inv = work.tile([P, BANK_UNITS], F32)
-                nc.vector.reciprocal(out=d_inv[:, 0 : len(units)], in_=o_ps[:, 0 : len(units), D])
-                for slot, unit in enumerate(units):
-                    h = unit % H
-                    nc.vector.scalar_tensor_tensor(
-                        out=om_sb[:, unit // H, D * h : D * (h + 1)],
-                        in0=o_ps[:, slot, 0:D],
-                        scalar=d_inv[:, slot : slot + 1],
-                        in1=q_of[b][:, h, a0 + unit // H, :],
-                        op0=MULT,
-                        op1=ADD,
-                    )
-            om_of[pair] = om_sb
+            o_ps = to_vector.tile([P, BANK_UNITS, D + 1], F32)
+            for slot, unit in enumerate(units):
+                nc.tensor.matmul(
+                    o_ps[:, slot, :],
+                    lhsT=qt_of[pair][:, unit, :],
+                    rhs=ctx_of[b][:, unit % H, 0 : D + 1],
+                    start=True,
+                    stop=True,
+                )
+            d_inv = work.tile([P, BANK_UNITS], F32)
+            nc.vector.reciprocal(out=d_inv[:, 0 : len(units)], in_=o_ps[:, 0 : len(units), D])
+            product_of[bank] = (o_ps, d_inv)
+
+        def normalise(bank):
+            pair, units = units_of(bank)
+            b, a0 = where(pair)
+            if bank % PAIR_BANKS == 0:
+                om_sb = work.tile([P, PAIR, E], BF16)
+                om_of[pair] = om_sb
+            o_ps, d_inv = product_of[bank]
+            for slot, unit in enumerate(units):
+                h = unit % H
+                nc.vector.scalar_tensor_tensor(
+                    out=om_of[pair][:, unit // H, D * h : D * (h + 1)],
+                    in0=o_ps[:, slot, 0:D],
+                    scalar=d_inv[:, slot : slot + 1],
+                    in1=q_of[b][:, h, a0 + unit // H, :],
+                    op0=MULT,
+                    op1=ADD,
+                )
 
         def transpose_om(pair):
             quad, half = pair // PAIRS_IN_QUAD, pair % PAIRS_IN_QUAD
             if half == 0:
                 grouped = work.tile([P, QUAD * P * PACK], BF16, align_bytes=64)
                 grouped_of[quad] = grouped
-            omt_ps = psum_omt.tile([P, PAIR, 2, P], F32)
+            omt_ps = to_scalar.tile([P, PAIR, 2, P], F32, tag="to_scalar")
             for tile_in_pair in range(PAIR):
                 om_words = om_of[pair][:, tile_in_pair, :].bitcast(F32)
                 for u in range(2):
@@ -143,7 +157,7 @@ def tile_linearattention_pb_t_kernel(tc, q, k_sum, context, Wp_words, Wp_scales,
 
         def project(quad):
             codes, scales = codes_of[quad]
-            out_ps = psum_out.tile([P, QUAD, DIM], F32)
+            out_ps = to_scalar.tile([P, QUAD, DIM], F32, tag="to_scalar")
             for i in range(QUAD):
                 nc.tensor.matmul_mx(
                     out=out_ps[:, i, :],
@@ -165,14 +179,15 @@ def tile_linearattention_pb_t_kernel(tc, q, k_sum, context, Wp_words, Wp_scales,
                 out=out[b].rearrange("(p a) n -> p a n", a=TILES)[:, a0 : a0 + QUAD, :], in_=result[:]
             )
 
+        def last_of_quad(pair):
+            return 0 <= pair < PAIRS and pair % PAIRS_IN_QUAD == PAIRS_IN_QUAD - 1
+
         load_batch(0)
 
         w_codes = const.tile([P, PACK * DIM], U8, align_bytes=64)
         nc.sync.dma_start(
             out=w_codes[:].bitcast(I32), in_=Wp_words[0].rearrange("p n j -> p (n j)").bitcast(I32)
         )
-        w_scales = const.tile([P, DIM], U8, align_bytes=64)
-        nc.vector.memset(w_scales[:].bitcast(I32), 0)
         for quadrant in range(4):
             nc.sync.dma_start(
                 out=w_scales[32 * quadrant : 32 * quadrant + 4, :].bitcast(I32),
@@ -182,20 +197,27 @@ def tile_linearattention_pb_t_kernel(tc, q, k_sum, context, Wp_words, Wp_scales,
         bias_bf16 = const.tile([P, DIM], BF16)
         nc.sync.dma_start(out=bias_bf16[:], in_=bp.partition_broadcast(P))
         bias = const.tile([P, DIM], F32)
-        nc.vector.tensor_copy(out=bias[:], in_=bias_bf16[:])
+        nc.gpsimd.tensor_copy(out=bias[:], in_=bias_bf16[:])
 
         for b in range(1, AHEAD):
             load_batch(b)
-        for step in range(PAIRS + 4):
+
+        transpose_q(0)
+        transpose_q(1)
+        for step in range(PAIRS + 5):
             if step % PAIRS_IN_BATCH == 0 and step // PAIRS_IN_BATCH + AHEAD < B:
                 load_batch(step // PAIRS_IN_BATCH + AHEAD)
-            if step < PAIRS:
-                transpose_q(step)
-            if 0 <= step - 1 < PAIRS:
-                attend(step - 1)
-            if 0 <= step - 2 < PAIRS:
-                transpose_om(step - 2)
-            if 0 <= step - 3 < PAIRS and (step - 3) % PAIRS_IN_QUAD == PAIRS_IN_QUAD - 1:
-                quantise((step - 3) // PAIRS_IN_QUAD)
-            if 0 <= step - 4 < PAIRS and (step - 4) % PAIRS_IN_QUAD == PAIRS_IN_QUAD - 1:
-                project((step - 4) // PAIRS_IN_QUAD)
+            for part in range(PAIR_BANKS):
+                bank = PAIR_BANKS * step + part
+                if bank < PAIR_BANKS * PAIRS:
+                    multiply(bank)
+                if 0 <= bank - 1 < PAIR_BANKS * PAIRS:
+                    normalise(bank - 1)
+                if part == 0 and step + 2 < PAIRS:
+                    transpose_q(step + 2)
+                if part == 1 and 0 <= step - 2 < PAIRS:
+                    transpose_om(step - 2)
+                if part == 2 and last_of_quad(step - 3):
+                    quantise((step - 3) // PAIRS_IN_QUAD)
+                if part == 2 and last_of_quad(step - 4):
+                    project((step - 4) // PAIRS_IN_QUAD)

@@ -27,6 +27,8 @@ PAIRS_IN_BATCH = TILES // PAIR
 PAIRS_IN_QUAD = QUAD // PAIR
 BANK_UNITS = 3
 PAIR_BANKS = 3
+FIRST_UNITS = PAIR_UNITS - BANK_UNITS * (PAIR_BANKS - 1)
+COPY = mybir.ActivationFunctionType.Copy
 CTX_PITCH = 144
 AHEAD = 3
 
@@ -40,8 +42,8 @@ def tile_linearattention_pb_t_kernel(tc, q, k_sum, context, Wp_words, Wp_scales,
         const = stack.enter_context(tc.tile_pool(name="const", bufs=1))
         batch_pool = stack.enter_context(tc.tile_pool(name="batch", bufs=AHEAD + 2))
         work = stack.enter_context(tc.tile_pool(name="work", bufs=4))
-        to_vector = stack.enter_context(tc.psum_pool(name="to_vector", bufs=4))
-        to_scalar = stack.enter_context(tc.psum_pool(name="to_scalar", bufs=4))
+        to_vector = stack.enter_context(tc.psum_pool(name="to_vector", bufs=3))
+        to_scalar = stack.enter_context(tc.psum_pool(name="to_scalar", bufs=5))
 
         w_scales = const.tile([P, DIM], U8, align_bytes=64)
         nc.vector.memset(w_scales[:].bitcast(I32), 0)
@@ -85,8 +87,9 @@ def tile_linearattention_pb_t_kernel(tc, q, k_sum, context, Wp_words, Wp_scales,
             return pair // PAIRS_IN_BATCH, PAIR * (pair % PAIRS_IN_BATCH)
 
         def units_of(bank):
-            first = BANK_UNITS * (bank % PAIR_BANKS)
-            return bank // PAIR_BANKS, list(range(first, min(first + BANK_UNITS, PAIR_UNITS)))
+            part = bank % PAIR_BANKS
+            first = 0 if part == 0 else FIRST_UNITS + BANK_UNITS * (part - 1)
+            return bank // PAIR_BANKS, list(range(first, FIRST_UNITS + BANK_UNITS * part))
 
         def transpose_q(pair):
             b, a0 = where(pair)
@@ -99,8 +102,11 @@ def tile_linearattention_pb_t_kernel(tc, q, k_sum, context, Wp_words, Wp_scales,
 
         def multiply(bank):
             pair, units = units_of(bank)
-            b, a0 = where(pair)
-            o_ps = to_vector.tile([P, BANK_UNITS, D + 1], F32)
+            b = pair // PAIRS_IN_BATCH
+            if bank % PAIR_BANKS == 0:
+                o_ps = to_scalar.tile([P, BANK_UNITS, D + 1], F32, tag="to_scalar")
+            else:
+                o_ps = to_vector.tile([P, BANK_UNITS, D + 1], F32, tag="to_vector")
             for slot, unit in enumerate(units):
                 nc.tensor.matmul(
                     o_ps[:, slot, :],
@@ -113,12 +119,27 @@ def tile_linearattention_pb_t_kernel(tc, q, k_sum, context, Wp_words, Wp_scales,
             nc.vector.reciprocal(out=d_inv[:, 0 : len(units)], in_=o_ps[:, 0 : len(units), D])
             product_of[bank] = (o_ps, d_inv)
 
+        def normalise_first(bank):
+            pair = bank // PAIR_BANKS
+            b, a0 = where(pair)
+            om_sb = work.tile([P, PAIR, E], BF16)
+            om_of[pair] = om_sb
+            o_ps, d_inv = product_of[bank]
+            scaled = work.tile([P, FIRST_UNITS, D], F32)
+            for slot in range(FIRST_UNITS):
+                nc.scalar.activation(
+                    out=scaled[:, slot, :], in_=o_ps[:, slot, 0:D], func=COPY, scale=d_inv[:, slot : slot + 1]
+                )
+            nc.gpsimd.tensor_tensor(
+                out=om_sb[:, 0, 0 : FIRST_UNITS * D].rearrange("p (h e) -> p h e", h=FIRST_UNITS),
+                in0=scaled[:],
+                in1=q_of[b][:, 0:FIRST_UNITS, a0, :],
+                op=ADD,
+            )
+
         def normalise(bank):
             pair, units = units_of(bank)
             b, a0 = where(pair)
-            if bank % PAIR_BANKS == 0:
-                om_sb = work.tile([P, PAIR, E], BF16)
-                om_of[pair] = om_sb
             o_ps, d_inv = product_of[bank]
             for slot, unit in enumerate(units):
                 h = unit % H
@@ -207,17 +228,22 @@ def tile_linearattention_pb_t_kernel(tc, q, k_sum, context, Wp_words, Wp_scales,
         for step in range(PAIRS + 5):
             if step % PAIRS_IN_BATCH == 0 and step // PAIRS_IN_BATCH + AHEAD < B:
                 load_batch(step // PAIRS_IN_BATCH + AHEAD)
-            for part in range(PAIR_BANKS):
-                bank = PAIR_BANKS * step + part
-                if bank < PAIR_BANKS * PAIRS:
-                    multiply(bank)
-                if 0 <= bank - 1 < PAIR_BANKS * PAIRS:
-                    normalise(bank - 1)
-                if part == 0 and step + 2 < PAIRS:
-                    transpose_q(step + 2)
-                if part == 1 and 0 <= step - 2 < PAIRS:
-                    transpose_om(step - 2)
-                if part == 2 and last_of_quad(step - 3):
-                    quantise((step - 3) // PAIRS_IN_QUAD)
-                if part == 2 and last_of_quad(step - 4):
-                    project((step - 4) // PAIRS_IN_QUAD)
+            first_bank = PAIR_BANKS * step
+            if step < PAIRS:
+                multiply(first_bank)
+                normalise_first(first_bank)
+            if step + 2 < PAIRS:
+                transpose_q(step + 2)
+            if step < PAIRS:
+                multiply(first_bank + 1)
+            if 0 <= step - 1 < PAIRS:
+                normalise(first_bank - 1)
+            if 0 <= step - 2 < PAIRS:
+                transpose_om(step - 2)
+            if step < PAIRS:
+                multiply(first_bank + 2)
+                normalise(first_bank + 1)
+            if last_of_quad(step - 3):
+                quantise((step - 3) // PAIRS_IN_QUAD)
+            if last_of_quad(step - 4):
+                project((step - 4) // PAIRS_IN_QUAD)

@@ -27,8 +27,6 @@ PAIRS_IN_BATCH = TILES // PAIR
 PAIRS_IN_QUAD = QUAD // PAIR
 BANK_UNITS = 3
 PAIR_BANKS = 3
-FIRST_UNITS = PAIR_UNITS - BANK_UNITS * (PAIR_BANKS - 1)
-COPY = mybir.ActivationFunctionType.Copy
 CTX_PITCH = 144
 AHEAD = 3
 
@@ -42,8 +40,8 @@ def tile_linearattention_pb_t_kernel(tc, q, k_sum, context, Wp_words, Wp_scales,
         const = stack.enter_context(tc.tile_pool(name="const", bufs=1))
         batch_pool = stack.enter_context(tc.tile_pool(name="batch", bufs=AHEAD + 2))
         work = stack.enter_context(tc.tile_pool(name="work", bufs=4))
-        to_vector = stack.enter_context(tc.psum_pool(name="to_vector", bufs=3))
-        to_scalar = stack.enter_context(tc.psum_pool(name="to_scalar", bufs=5))
+        to_vector = stack.enter_context(tc.psum_pool(name="to_vector", bufs=4))
+        to_scalar = stack.enter_context(tc.psum_pool(name="to_scalar", bufs=4))
 
         w_scales = const.tile([P, DIM], U8, align_bytes=64)
         nc.vector.memset(w_scales[:].bitcast(I32), 0)
@@ -87,9 +85,8 @@ def tile_linearattention_pb_t_kernel(tc, q, k_sum, context, Wp_words, Wp_scales,
             return pair // PAIRS_IN_BATCH, PAIR * (pair % PAIRS_IN_BATCH)
 
         def units_of(bank):
-            part = bank % PAIR_BANKS
-            first = 0 if part == 0 else FIRST_UNITS + BANK_UNITS * (part - 1)
-            return bank // PAIR_BANKS, list(range(first, FIRST_UNITS + BANK_UNITS * part))
+            first = BANK_UNITS * (bank % PAIR_BANKS)
+            return bank // PAIR_BANKS, list(range(first, min(first + BANK_UNITS, PAIR_UNITS)))
 
         def transpose_q(pair):
             b, a0 = where(pair)
@@ -97,16 +94,13 @@ def tile_linearattention_pb_t_kernel(tc, q, k_sum, context, Wp_words, Wp_scales,
             for unit in range(PAIR_UNITS):
                 nc.tensor.transpose(qt_ps[:, unit, :], q_of[b][:, unit % H, a0 + unit // H, :], ident_bf16[:])
             qt_sb = work.tile([P, PAIR_UNITS, P], BF16)
-            nc.scalar.copy(out=qt_sb[:], in_=qt_ps[:])
+            nc.scalar.copy(out=qt_sb[:].bitcast(F32), in_=qt_ps[:].bitcast(F32))
             qt_of[pair] = qt_sb
 
         def multiply(bank):
             pair, units = units_of(bank)
-            b = pair // PAIRS_IN_BATCH
-            if bank % PAIR_BANKS == 0:
-                o_ps = to_scalar.tile([P, BANK_UNITS, D + 1], F32, tag="to_scalar")
-            else:
-                o_ps = to_vector.tile([P, BANK_UNITS, D + 1], F32, tag="to_vector")
+            b, a0 = where(pair)
+            o_ps = to_vector.tile([P, BANK_UNITS, D + 1], F32)
             for slot, unit in enumerate(units):
                 nc.tensor.matmul(
                     o_ps[:, slot, :],
@@ -119,27 +113,12 @@ def tile_linearattention_pb_t_kernel(tc, q, k_sum, context, Wp_words, Wp_scales,
             nc.vector.reciprocal(out=d_inv[:, 0 : len(units)], in_=o_ps[:, 0 : len(units), D])
             product_of[bank] = (o_ps, d_inv)
 
-        def normalise_first(bank):
-            pair = bank // PAIR_BANKS
-            b, a0 = where(pair)
-            om_sb = work.tile([P, PAIR, E], BF16)
-            om_of[pair] = om_sb
-            o_ps, d_inv = product_of[bank]
-            scaled = work.tile([P, FIRST_UNITS, D], F32)
-            for slot in range(FIRST_UNITS):
-                nc.scalar.activation(
-                    out=scaled[:, slot, :], in_=o_ps[:, slot, 0:D], func=COPY, scale=d_inv[:, slot : slot + 1]
-                )
-            nc.gpsimd.tensor_tensor(
-                out=om_sb[:, 0, 0 : FIRST_UNITS * D].rearrange("p (h e) -> p h e", h=FIRST_UNITS),
-                in0=scaled[:],
-                in1=q_of[b][:, 0:FIRST_UNITS, a0, :],
-                op=ADD,
-            )
-
         def normalise(bank):
             pair, units = units_of(bank)
             b, a0 = where(pair)
+            if bank % PAIR_BANKS == 0:
+                om_sb = work.tile([P, PAIR, E], BF16)
+                om_of[pair] = om_sb
             o_ps, d_inv = product_of[bank]
             for slot, unit in enumerate(units):
                 h = unit % H
@@ -228,22 +207,17 @@ def tile_linearattention_pb_t_kernel(tc, q, k_sum, context, Wp_words, Wp_scales,
         for step in range(PAIRS + 5):
             if step % PAIRS_IN_BATCH == 0 and step // PAIRS_IN_BATCH + AHEAD < B:
                 load_batch(step // PAIRS_IN_BATCH + AHEAD)
-            first_bank = PAIR_BANKS * step
-            if step < PAIRS:
-                multiply(first_bank)
-                normalise_first(first_bank)
-            if step + 2 < PAIRS:
-                transpose_q(step + 2)
-            if step < PAIRS:
-                multiply(first_bank + 1)
-            if 0 <= step - 1 < PAIRS:
-                normalise(first_bank - 1)
-            if 0 <= step - 2 < PAIRS:
-                transpose_om(step - 2)
-            if step < PAIRS:
-                multiply(first_bank + 2)
-                normalise(first_bank + 1)
-            if last_of_quad(step - 3):
-                quantise((step - 3) // PAIRS_IN_QUAD)
-            if last_of_quad(step - 4):
-                project((step - 4) // PAIRS_IN_QUAD)
+            for part in range(PAIR_BANKS):
+                bank = PAIR_BANKS * step + part
+                if bank < PAIR_BANKS * PAIRS:
+                    multiply(bank)
+                if 0 <= bank - 1 < PAIR_BANKS * PAIRS:
+                    normalise(bank - 1)
+                if part == 0 and step + 2 < PAIRS:
+                    transpose_q(step + 2)
+                if part == 1 and 0 <= step - 2 < PAIRS:
+                    transpose_om(step - 2)
+                if part == 2 and last_of_quad(step - 3):
+                    quantise((step - 3) // PAIRS_IN_QUAD)
+                if part == 2 and last_of_quad(step - 4):
+                    project((step - 4) // PAIRS_IN_QUAD)

@@ -219,5 +219,5 @@ def tile_linearattention_pb_t_kernel(tc, q, k_sum, context, Wp_words, Wp_scales,
                     transpose_om(step - 2)
                 if part == 2 and last_of_quad(step - 3):
                     quantise((step - 3) // PAIRS_IN_QUAD)
-                if part == 2 and last_of_quad(step - 4):
-                    project((step - 4) // PAIRS_IN_QUAD)
+                if part == 2 and last_of_quad(step - 5):
+                    project((step - 5) // PAIRS_IN_QUAD)

@@ -40,8 +40,8 @@ def tile_linearattention_pb_t_kernel(tc, q, k_sum, context, Wp_words, Wp_scales,
         const = stack.enter_context(tc.tile_pool(name="const", bufs=1))
         batch_pool = stack.enter_context(tc.tile_pool(name="batch", bufs=AHEAD + 2))
         work = stack.enter_context(tc.tile_pool(name="work", bufs=4))
-        to_vector = stack.enter_context(tc.psum_pool(name="to_vector", bufs=4))
-        to_scalar = stack.enter_context(tc.psum_pool(name="to_scalar", bufs=4))
+        to_vector = stack.enter_context(tc.psum_pool(name="to_vector", bufs=5))
+        to_scalar = stack.enter_context(tc.psum_pool(name="to_scalar", bufs=3))
 
         w_scales = const.tile([P, DIM], U8, align_bytes=64)
         nc.vector.memset(w_scales[:].bitcast(I32), 0)

@@ -67,16 +67,20 @@ def tile_linearattention_pb_t_kernel(tc, q, k_sum, context, Wp_words, Wp_scales,
         grouped_of = {}
         codes_of = {}
 
-        def load_batch(b):
+        def load_batch(b, pieces):
             ctx_sb = batch_pool.tile([P, H, CTX_PITCH], BF16)
-            nc.sync.dma_start(out=ctx_sb[:, :, 0:D], in_=context[b].rearrange("h d e -> d h e"))
+            q_sb = batch_pool.tile([P, H, TILES, D], BF16)
+            width = TILES // pieces
+            for piece in range(pieces):
+                if piece == min(1, pieces - 1):
+                    nc.sync.dma_start(out=ctx_sb[:, :, 0:D], in_=context[b].rearrange("h d e -> d h e"))
+                tiles = slice(width * piece, width * (piece + 1))
+                nc.sync.dma_start(
+                    out=q_sb[:, :, tiles, :].rearrange("p h a d -> p h (a d)"),
+                    in_=q[b].rearrange("h (p a) d -> p h a d", a=TILES)[:, :, tiles, :].rearrange("p h a d -> p h (a d)"),
+                )
             nc.gpsimd.tensor_copy(
                 out=ctx_sb[:, :, D : D + 1], in_=ksum_cols[:, H * b : H * (b + 1)].unsqueeze(2)
-            )
-            q_sb = batch_pool.tile([P, H, TILES, D], BF16)
-            nc.sync.dma_start(
-                out=q_sb[:].rearrange("p h a d -> p h (a d)"),
-                in_=q[b].rearrange("h (p a) d -> p h (a d)", a=TILES),
             )
             ctx_of[b] = ctx_sb
             q_of[b] = q_sb
@@ -182,7 +186,8 @@ def tile_linearattention_pb_t_kernel(tc, q, k_sum, context, Wp_words, Wp_scales,
         def last_of_quad(pair):
             return 0 <= pair < PAIRS and pair % PAIRS_IN_QUAD == PAIRS_IN_QUAD - 1
 
-        load_batch(0)
+        load_batch(0, PAIRS_IN_BATCH)
+        load_batch(1, 1)
 
         w_codes = const.tile([P, PACK * DIM], U8, align_bytes=64)
         nc.sync.dma_start(
@@ -199,14 +204,14 @@ def tile_linearattention_pb_t_kernel(tc, q, k_sum, context, Wp_words, Wp_scales,
         bias = const.tile([P, DIM], F32)
         nc.gpsimd.tensor_copy(out=bias[:], in_=bias_bf16[:])
 
-        for b in range(1, AHEAD):
-            load_batch(b)
+        for b in range(2, AHEAD):
+            load_batch(b, 1)
 
         transpose_q(0)
         transpose_q(1)
         for step in range(PAIRS + 5):
             if step % PAIRS_IN_BATCH == 0 and step // PAIRS_IN_BATCH + AHEAD < B:
-                load_batch(step // PAIRS_IN_BATCH + AHEAD)
+                load_batch(step // PAIRS_IN_BATCH + AHEAD, 1)
             for part in range(PAIR_BANKS):
                 bank = PAIR_BANKS * step + part
                 if bank < PAIR_BANKS * PAIRS:

@@ -25,6 +25,7 @@ QUAD = 4
 PAIRS = B * TILES // PAIR
 PAIRS_IN_BATCH = TILES // PAIR
 PAIRS_IN_QUAD = QUAD // PAIR
+QUADS = PAIRS // PAIRS_IN_QUAD
 BANK_UNITS = 3
 PAIR_BANKS = 3
 CTX_PITCH = 144
@@ -43,6 +44,31 @@ def tile_linearattention_pb_t_kernel(tc, q, k_sum, context, Wp_words, Wp_scales,
         to_vector = stack.enter_context(tc.psum_pool(name="to_vector", bufs=5))
         to_scalar = stack.enter_context(tc.psum_pool(name="to_scalar", bufs=3))
 
+        q_of = {}
+        ctx_of = {}
+
+        def load_batch(b, pieces):
+            ctx_sb = batch_pool.tile([P, H, CTX_PITCH], BF16)
+            q_sb = batch_pool.tile([P, H, TILES, D], BF16)
+            width = TILES // pieces
+            for piece in range(pieces):
+                if piece == min(1, pieces - 1):
+                    if b == 0:
+                        nc.sync.dma_start(out=ksum_rows[0 : B * H, :], in_=k_sum.rearrange("b h o d -> (b h o) d"))
+                    nc.sync.dma_start(out=ctx_sb[:, :, 0:D], in_=context[b].rearrange("h d e -> d h e"))
+                tiles = slice(width * piece, width * (piece + 1))
+                nc.sync.dma_start(
+                    out=q_sb[:, :, tiles, :].rearrange("p h a d -> p h (a d)"),
+                    in_=q[b].rearrange("h (p a) d -> p h a d", a=TILES)[:, :, tiles, :].rearrange("p h a d -> p h (a d)"),
+                )
+            ctx_of[b] = ctx_sb
+            q_of[b] = q_sb
+
+        ksum_rows = const.tile([P, D], BF16)
+        nc.vector.memset(ksum_rows[:], 0.0)
+        load_batch(0, PAIRS_IN_BATCH)
+        load_batch(1, 1)
+
         w_scales = const.tile([P, DIM], U8, align_bytes=64)
         nc.vector.memset(w_scales[:].bitcast(I32), 0)
 
@@ -51,39 +77,12 @@ def tile_linearattention_pb_t_kernel(tc, q, k_sum, context, Wp_words, Wp_scales,
         ident_f32 = const.tile([P, P], F32)
         make_identity(nc, ident_f32[:])
 
-        ksum_rows = const.tile([P, D], BF16)
-        nc.vector.memset(ksum_rows[:], 0.0)
-        nc.sync.dma_start(out=ksum_rows[0 : B * H, :], in_=k_sum.rearrange("b h o d -> (b h o) d"))
-        ksum_ps = to_scalar.tile([P, PAIR_UNITS, P], BF16, tag="to_scalar")
-        nc.tensor.transpose(ksum_ps[:, 0, :], ksum_rows[:], ident_bf16[:])
-        ksum_cols = const.tile([P, B * H], BF16)
-        nc.scalar.copy(out=ksum_cols[:], in_=ksum_ps[:, 0, 0 : B * H])
-
-        q_of = {}
-        ctx_of = {}
         qt_of = {}
         product_of = {}
         om_of = {}
         grouped_of = {}
         codes_of = {}
-
-        def load_batch(b, pieces):
-            ctx_sb = batch_pool.tile([P, H, CTX_PITCH], BF16)
-            q_sb = batch_pool.tile([P, H, TILES, D], BF16)
-            width = TILES // pieces
-            for piece in range(pieces):
-                if piece == min(1, pieces - 1):
-                    nc.sync.dma_start(out=ctx_sb[:, :, 0:D], in_=context[b].rearrange("h d e -> d h e"))
-                tiles = slice(width * piece, width * (piece + 1))
-                nc.sync.dma_start(
-                    out=q_sb[:, :, tiles, :].rearrange("p h a d -> p h (a d)"),
-                    in_=q[b].rearrange("h (p a) d -> p h a d", a=TILES)[:, :, tiles, :].rearrange("p h a d -> p h (a d)"),
-                )
-            nc.gpsimd.tensor_copy(
-                out=ctx_sb[:, :, D : D + 1], in_=ksum_cols[:, H * b : H * (b + 1)].unsqueeze(2)
-            )
-            ctx_of[b] = ctx_sb
-            q_of[b] = q_sb
+        out_ps_of = {}
 
         def where(pair):
             return pair // PAIRS_IN_BATCH, PAIR * (pair % PAIRS_IN_BATCH)
@@ -104,7 +103,7 @@ def tile_linearattention_pb_t_kernel(tc, q, k_sum, context, Wp_words, Wp_scales,
         def multiply(bank):
             pair, units = units_of(bank)
             b, a0 = where(pair)
-            o_ps = to_vector.tile([P, BANK_UNITS, D + 1], F32)
+            o_ps = to_vector.tile([P, BANK_UNITS, D + 1], F32, tag="to_vector")
             for slot, unit in enumerate(units):
                 nc.tensor.matmul(
                     o_ps[:, slot, :],
@@ -135,36 +134,44 @@ def tile_linearattention_pb_t_kernel(tc, q, k_sum, context, Wp_words, Wp_scales,
                     op1=ADD,
                 )
 
-        def transpose_om(pair):
+        def transpose_om(pair, tiles):
             quad, half = pair // PAIRS_IN_QUAD, pair % PAIRS_IN_QUAD
-            if half == 0:
+            if half == 0 and tiles[0] == 0:
                 grouped = work.tile([P, QUAD * P * PACK], BF16, align_bytes=64)
                 grouped_of[quad] = grouped
             omt_ps = to_scalar.tile([P, PAIR, 2, P], F32, tag="to_scalar")
-            for tile_in_pair in range(PAIR):
+            for slot, tile_in_pair in enumerate(tiles):
                 om_words = om_of[pair][:, tile_in_pair, :].bitcast(F32)
                 for u in range(2):
-                    nc.tensor.transpose(omt_ps[:, tile_in_pair, u, :], om_words[:, u : E // 2 : 2], ident_f32[:])
-            words = PAIR * P * 2
+                    nc.tensor.transpose(omt_ps[:, slot, u, :], om_words[:, u : E // 2 : 2], ident_f32[:])
+            words = P * 2
+            first = PAIR * half + tiles[0]
             nc.scalar.copy(
                 out=grouped_of[quad][:]
-                .bitcast(F32)[:, words * half : words * (half + 1)]
-                .rearrange("p (i t u) -> p i t u", i=PAIR, u=2),
-                in_=omt_ps[:].rearrange("p i u t -> p i t u"),
+                .bitcast(F32)[:, words * first : words * (first + len(tiles))]
+                .rearrange("p (i t u) -> p i t u", i=len(tiles), u=2),
+                in_=omt_ps[:, 0 : len(tiles), :, :].rearrange("p i u t -> p i t u"),
             )
 
-        def quantise(quad):
-            codes = work.tile([P, QUAD * P], U32, align_bytes=64)
-            scales = work.tile([P, QUAD * P], U8, align_bytes=64)
-            nc.vector.quantize_mx(out=codes[:].bitcast(FP8X4), scales=scales[:], in_=grouped_of[quad][:])
-            codes_of[quad] = (codes, scales)
-
-        def project(quad):
+        def quantise(quad, first, count):
+            if first == 0:
+                codes = work.tile([P, QUAD * P], U32, align_bytes=64)
+                scales = work.tile([P, QUAD * P], U8, align_bytes=64)
+                codes_of[quad] = (codes, scales)
             codes, scales = codes_of[quad]
-            out_ps = to_scalar.tile([P, QUAD, DIM], F32, tag="to_scalar")
-            for i in range(QUAD):
+            tokens = slice(P * first, P * (first + count))
+            nc.vector.quantize_mx(
+                out=codes[:, tokens].bitcast(FP8X4),
+                scales=scales[:, tokens],
+                in_=grouped_of[quad][:, PACK * P * first : PACK * P * (first + count)],
+            )
+
+        def project(quad, first, count, ring):
+            codes, scales = codes_of[quad]
+            out_ps = ring.tile([P, QUAD, DIM], F32, tag="to_vector" if ring is to_vector else "to_scalar")
+            for i in range(first, first + count):
                 nc.tensor.matmul_mx(
-                    out=out_ps[:, i, :],
+                    out=out_ps[:, i - first, :],
                     lhsT=codes[:, P * i : P * (i + 1)].bitcast(FP8X4),
                     lhsT_scale=scales[:, P * i : P * (i + 1)],
                     rhs=w_codes[:].bitcast(FP8X4),
@@ -172,22 +179,27 @@ def tile_linearattention_pb_t_kernel(tc, q, k_sum, context, Wp_words, Wp_scales,
                     start=True,
                     stop=True,
                 )
-            no_bias = work.tile([P, QUAD, DIM], F32)
-            nc.scalar.copy(out=no_bias[:], in_=out_ps[:])
-            result = work.tile([P, QUAD, DIM], F32)
-            nc.gpsimd.tensor_tensor(
-                out=result[:], in0=no_bias[:], in1=bias[:].unsqueeze(1).to_broadcast([P, QUAD, DIM]), op=ADD
-            )
+            out_ps_of[(quad, first)] = out_ps
+
+        def finish(quad, first, count, on_vector):
+            out_ps = out_ps_of[(quad, first)]
+            bias_rows = bias[:].unsqueeze(1).to_broadcast([P, count, DIM])
+            if on_vector:
+                result = work.tile([P, QUAD, DIM], F32, tag="result_of_vector")
+                nc.vector.tensor_tensor(out=result[:, 0:count, :], in0=out_ps[:, 0:count, :], in1=bias_rows, op=ADD)
+            else:
+                result = work.tile([P, QUAD, DIM], F32, tag="result_of_gpsimd")
+                no_bias = work.tile([P, QUAD, DIM], F32)
+                nc.scalar.copy(out=no_bias[:, 0:count, :], in_=out_ps[:, 0:count, :])
+                nc.gpsimd.tensor_tensor(out=result[:, 0:count, :], in0=no_bias[:, 0:count, :], in1=bias_rows, op=ADD)
             b, a0 = where(quad * PAIRS_IN_QUAD)
             nc.sync.dma_start(
-                out=out[b].rearrange("(p a) n -> p a n", a=TILES)[:, a0 : a0 + QUAD, :], in_=result[:]
+                out=out[b].rearrange("(p a) n -> p a n", a=TILES)[:, a0 + first : a0 + first + count, :],
+                in_=result[:, 0:count, :],
             )
 
         def last_of_quad(pair):
             return 0 <= pair < PAIRS and pair % PAIRS_IN_QUAD == PAIRS_IN_QUAD - 1
-
-        load_batch(0, PAIRS_IN_BATCH)
-        load_batch(1, 1)
 
         w_codes = const.tile([P, PACK * DIM], U8, align_bytes=64)
         nc.sync.dma_start(
@@ -201,28 +213,59 @@ def tile_linearattention_pb_t_kernel(tc, q, k_sum, context, Wp_words, Wp_scales,
 
         bias_bf16 = const.tile([P, DIM], BF16)
         nc.sync.dma_start(out=bias_bf16[:], in_=bp.partition_broadcast(P))
-        bias = const.tile([P, DIM], F32)
-        nc.gpsimd.tensor_copy(out=bias[:], in_=bias_bf16[:])
 
         for b in range(2, AHEAD):
             load_batch(b, 1)
 
         transpose_q(0)
+
+        ksum_ps = to_scalar.tile([P, PAIR_UNITS, P], BF16, tag="to_scalar")
+        nc.tensor.transpose(ksum_ps[:, 0, :], ksum_rows[:], ident_bf16[:])
+        ksum_cols = const.tile([P, B * H], BF16)
+        nc.scalar.copy(out=ksum_cols[:], in_=ksum_ps[:, 0, 0 : B * H])
+
+        def add_k_sum(b):
+            nc.gpsimd.tensor_copy(
+                out=ctx_of[b][:, :, D : D + 1], in_=ksum_cols[:, H * b : H * (b + 1)].unsqueeze(2)
+            )
+
+        for b in range(AHEAD):
+            add_k_sum(b)
+        bias = const.tile([P, DIM], F32)
+        nc.gpsimd.tensor_copy(out=bias[:], in_=bias_bf16[:])
         transpose_q(1)
-        for step in range(PAIRS + 5):
+        for step in range(PAIRS):
             if step % PAIRS_IN_BATCH == 0 and step // PAIRS_IN_BATCH + AHEAD < B:
                 load_batch(step // PAIRS_IN_BATCH + AHEAD, 1)
+                add_k_sum(step // PAIRS_IN_BATCH + AHEAD)
             for part in range(PAIR_BANKS):
                 bank = PAIR_BANKS * step + part
-                if bank < PAIR_BANKS * PAIRS:
-                    multiply(bank)
-                if 0 <= bank - 1 < PAIR_BANKS * PAIRS:
+                multiply(bank)
+                if bank >= 1:
                     normalise(bank - 1)
                 if part == 0 and step + 2 < PAIRS:
                     transpose_q(step + 2)
-                if part == 1 and 0 <= step - 2 < PAIRS:
-                    transpose_om(step - 2)
+                if part == 1 and step >= 2:
+                    transpose_om(step - 2, [0, 1])
                 if part == 2 and last_of_quad(step - 3):
-                    quantise((step - 3) // PAIRS_IN_QUAD)
+                    quantise((step - 3) // PAIRS_IN_QUAD, 0, QUAD)
                 if part == 2 and last_of_quad(step - 5):
-                    project((step - 5) // PAIRS_IN_QUAD)
+                    project((step - 5) // PAIRS_IN_QUAD, 0, QUAD, to_scalar)
+                    finish((step - 5) // PAIRS_IN_QUAD, 0, QUAD, False)
+
+        last = QUADS - 1
+        normalise(PAIR_BANKS * PAIRS - 1)
+        transpose_om(PAIRS - 2, [0, 1])
+        transpose_om(PAIRS - 1, [0])
+        project(last - 2, 0, QUAD, to_scalar)
+        transpose_om(PAIRS - 1, [1])
+        quantise(last - 1, 0, QUAD)
+        project(last - 1, 0, QUAD, to_vector)
+        pieces = [(0, PAIR), (PAIR, 1), (PAIR + 1, 1)]
+        for first, count in pieces:
+            quantise(last, first, count)
+            project(last, first, count, to_vector)
+        finish(last - 2, 0, QUAD, False)
+        finish(last - 1, 0, QUAD, True)
+        for first, count in pieces:
+            finish(last, first, count, True)

@@ -116,6 +116,9 @@ def tile_linearattention_pb_t_kernel(tc, q, k_sum, context, Wp_words, Wp_scales,
             nc.vector.reciprocal(out=d_inv[:, 0 : len(units)], in_=o_ps[:, 0 : len(units), D])
             product_of[bank] = (o_ps, d_inv)
 
+        def by_halves(pair, tile_in_pair):
+            return pair % PAIRS_IN_QUAD == 0 and tile_in_pair == 0
+
         def normalise(bank):
             pair, units = units_of(bank)
             b, a0 = where(pair)
@@ -125,14 +128,27 @@ def tile_linearattention_pb_t_kernel(tc, q, k_sum, context, Wp_words, Wp_scales,
             o_ps, d_inv = product_of[bank]
             for slot, unit in enumerate(units):
                 h = unit % H
-                nc.vector.scalar_tensor_tensor(
-                    out=om_of[pair][:, unit // H, D * h : D * (h + 1)],
-                    in0=o_ps[:, slot, 0:D],
-                    scalar=d_inv[:, slot : slot + 1],
-                    in1=q_of[b][:, h, a0 + unit // H, :],
-                    op0=MULT,
-                    op1=ADD,
-                )
+                if by_halves(pair, unit // H):
+                    for u in range(2):
+                        nc.vector.scalar_tensor_tensor(
+                            out=om_of[pair][:, unit // H, :].rearrange("p (u w s) -> p u w s", u=2, s=2)[
+                                :, u, (D // PACK) * h : (D // PACK) * (h + 1), :
+                            ],
+                            in0=o_ps[:, slot, 0:D].rearrange("p (w u s) -> p u w s", u=2, s=2)[:, u, :, :],
+                            scalar=d_inv[:, slot : slot + 1],
+                            in1=q_of[b][:, h, a0 + unit // H, :].rearrange("p (w u s) -> p u w s", u=2, s=2)[:, u, :, :],
+                            op0=MULT,
+                            op1=ADD,
+                        )
+                else:
+                    nc.vector.scalar_tensor_tensor(
+                        out=om_of[pair][:, unit // H, D * h : D * (h + 1)],
+                        in0=o_ps[:, slot, 0:D],
+                        scalar=d_inv[:, slot : slot + 1],
+                        in1=q_of[b][:, h, a0 + unit // H, :],
+                        op0=MULT,
+                        op1=ADD,
+                    )
 
         def transpose_om(pair, tiles):
             quad, half = pair // PAIRS_IN_QUAD, pair % PAIRS_IN_QUAD
@@ -143,7 +159,11 @@ def tile_linearattention_pb_t_kernel(tc, q, k_sum, context, Wp_words, Wp_scales,
             for slot, tile_in_pair in enumerate(tiles):
                 om_words = om_of[pair][:, tile_in_pair, :].bitcast(F32)
                 for u in range(2):
-                    nc.tensor.transpose(omt_ps[:, slot, u, :], om_words[:, u : E // 2 : 2], ident_f32[:])
+                    if by_halves(pair, tile_in_pair):
+                        words_of_u = om_words[:, P * u : P * (u + 1)]
+                    else:
+                        words_of_u = om_words[:, u : E // 2 : 2]
+                    nc.tensor.transpose(omt_ps[:, slot, u, :], words_of_u, ident_f32[:])
             words = P * 2
             first = PAIR * half + tiles[0]
             nc.scalar.copy(

@@ -116,9 +116,6 @@ def tile_linearattention_pb_t_kernel(tc, q, k_sum, context, Wp_words, Wp_scales,
             nc.vector.reciprocal(out=d_inv[:, 0 : len(units)], in_=o_ps[:, 0 : len(units), D])
             product_of[bank] = (o_ps, d_inv)
 
-        def by_halves(pair, tile_in_pair):
-            return pair % PAIRS_IN_QUAD == 0 and tile_in_pair == 0
-
         def normalise(bank):
             pair, units = units_of(bank)
             b, a0 = where(pair)
@@ -128,27 +125,16 @@ def tile_linearattention_pb_t_kernel(tc, q, k_sum, context, Wp_words, Wp_scales,
             o_ps, d_inv = product_of[bank]
             for slot, unit in enumerate(units):
                 h = unit % H
-                if by_halves(pair, unit // H):
-                    for u in range(2):
-                        nc.vector.scalar_tensor_tensor(
-                            out=om_of[pair][:, unit // H, :].rearrange("p (u w s) -> p u w s", u=2, s=2)[
-                                :, u, (D // PACK) * h : (D // PACK) * (h + 1), :
-                            ],
-                            in0=o_ps[:, slot, 0:D].rearrange("p (w u s) -> p u w s", u=2, s=2)[:, u, :, :],
-                            scalar=d_inv[:, slot : slot + 1],
-                            in1=q_of[b][:, h, a0 + unit // H, :].rearrange("p (w u s) -> p u w s", u=2, s=2)[:, u, :, :],
-                            op0=MULT,
-                            op1=ADD,
-                        )
-                else:
-                    nc.vector.scalar_tensor_tensor(
-                        out=om_of[pair][:, unit // H, D * h : D * (h + 1)],
-                        in0=o_ps[:, slot, 0:D],
-                        scalar=d_inv[:, slot : slot + 1],
-                        in1=q_of[b][:, h, a0 + unit // H, :],
-                        op0=MULT,
-                        op1=ADD,
-                    )
+                nc.vector.scalar_tensor_tensor(
+                    out=om_of[pair][:, unit // H, :].rearrange("p (u m) -> p u m", u=2)[
+                        :, :, (D // 2) * h : (D // 2) * (h + 1)
+                    ],
+                    in0=o_ps[:, slot, 0:D].rearrange("p (m u) -> p u m", u=2),
+                    scalar=d_inv[:, slot : slot + 1],
+                    in1=q_of[b][:, h, a0 + unit // H, :].rearrange("p (m u) -> p u m", u=2),
+                    op0=MULT,
+                    op1=ADD,
+                )
 
         def transpose_om(pair, tiles):
             quad, half = pair // PAIRS_IN_QUAD, pair % PAIRS_IN_QUAD
@@ -159,11 +145,7 @@ def tile_linearattention_pb_t_kernel(tc, q, k_sum, context, Wp_words, Wp_scales,
             for slot, tile_in_pair in enumerate(tiles):
                 om_words = om_of[pair][:, tile_in_pair, :].bitcast(F32)
                 for u in range(2):
-                    if by_halves(pair, tile_in_pair):
-                        words_of_u = om_words[:, P * u : P * (u + 1)]
-                    else:
-                        words_of_u = om_words[:, u : E // 2 : 2]
-                    nc.tensor.transpose(omt_ps[:, slot, u, :], words_of_u, ident_f32[:])
+                    nc.tensor.transpose(omt_ps[:, slot, u, :], om_words[:, P * u : P * (u + 1)], ident_f32[:])
             words = P * 2
             first = PAIR * half + tiles[0]
             nc.scalar.copy(
@@ -221,10 +203,11 @@ def tile_linearattention_pb_t_kernel(tc, q, k_sum, context, Wp_words, Wp_scales,
         def last_of_quad(pair):
             return 0 <= pair < PAIRS and pair % PAIRS_IN_QUAD == PAIRS_IN_QUAD - 1
 
-        w_codes = const.tile([P, PACK * DIM], U8, align_bytes=64)
+        w_as_it_comes = const.tile([P, PACK * DIM], U8, align_bytes=64)
         nc.sync.dma_start(
-            out=w_codes[:].bitcast(I32), in_=Wp_words[0].rearrange("p n j -> p (n j)").bitcast(I32)
+            out=w_as_it_comes[:].bitcast(I32), in_=Wp_words[0].rearrange("p n j -> p (n j)").bitcast(I32)
         )
+        w_codes = const.tile([P, PACK * DIM], U8, align_bytes=64)
         for quadrant in range(4):
             nc.sync.dma_start(
                 out=w_scales[32 * quadrant : 32 * quadrant + 4, :].bitcast(I32),
@@ -263,6 +246,11 @@ def tile_linearattention_pb_t_kernel(tc, q, k_sum, context, Wp_words, Wp_scales,
                 multiply(bank)
                 if bank >= 1:
                     normalise(bank - 1)
+                if step == 2 and part == 0:
+                    nc.vector.tensor_copy(
+                        out=w_codes[:].rearrange("p (n u s) -> p n s u", u=2, s=2),
+                        in_=w_as_it_comes[:].rearrange("p (n s u) -> p n s u", u=2, s=2),
+                    )
                 if part == 0 and step + 2 < PAIRS:
                     transpose_q(step + 2)
                 if part == 1 and step >= 2:

@@ -28,6 +28,7 @@ PAIRS_IN_QUAD = QUAD // PAIR
 QUADS = PAIRS // PAIRS_IN_QUAD
 BANK_UNITS = 3
 PAIR_BANKS = 3
+BANK_COLUMNS = 512
 CTX_PITCH = 144
 AHEAD = 3
 
@@ -79,6 +80,7 @@ def tile_linearattention_pb_t_kernel(tc, q, k_sum, context, Wp_words, Wp_scales,
 
         qt_of = {}
         product_of = {}
+        guest_d_inv_of = {}
         om_of = {}
         grouped_of = {}
         codes_of = {}
@@ -103,18 +105,39 @@ def tile_linearattention_pb_t_kernel(tc, q, k_sum, context, Wp_words, Wp_scales,
         def multiply(bank):
             pair, units = units_of(bank)
             b, a0 = where(pair)
-            o_ps = to_vector.tile([P, BANK_UNITS, D + 1], F32, tag="to_vector")
-            for slot, unit in enumerate(units):
+            o_ps = to_vector.tile([P, BANK_COLUMNS], F32, tag="to_vector")
+            if len(units) == BANK_UNITS:
+                guest = PAIR_BANKS * (BANK_UNITS - 1) + bank % PAIR_BANKS
+                for slot, unit in enumerate(units):
+                    nc.tensor.matmul(
+                        o_ps[:, 1 + (D + 1) * slot : 1 + (D + 1) * (slot + 1)],
+                        lhsT=qt_of[pair][:, unit, :],
+                        rhs=ctx_of[b][:, unit % H, 0 : D + 1],
+                        start=True,
+                        stop=True,
+                    )
                 nc.tensor.matmul(
-                    o_ps[:, slot, :],
-                    lhsT=qt_of[pair][:, unit, :],
-                    rhs=ctx_of[b][:, unit % H, 0 : D + 1],
+                    o_ps[:, 0:1],
+                    lhsT=qt_of[pair][:, guest, :],
+                    rhs=ctx_of[b][:, guest % H, D : D + 1],
                     start=True,
                     stop=True,
                 )
-            d_inv = work.tile([P, BANK_UNITS], F32)
-            nc.vector.reciprocal(out=d_inv[:, 0 : len(units)], in_=o_ps[:, 0 : len(units), D])
-            product_of[bank] = (o_ps, d_inv)
+                d_inv = work.tile([P, BANK_UNITS + 1], F32)
+                nc.vector.reciprocal(out=d_inv[:], in_=o_ps[:, 0 : (D + 1) * BANK_UNITS + 1 : D + 1])
+                for slot, unit in enumerate(units):
+                    product_of[(pair, unit)] = (o_ps[:, 1 + (D + 1) * slot : D + 1 + (D + 1) * slot], d_inv[:, slot + 1 : slot + 2])
+                guest_d_inv_of[(pair, guest)] = d_inv[:, 0:1]
+            else:
+                for slot, unit in enumerate(units):
+                    nc.tensor.matmul(
+                        o_ps[:, D * slot : D * (slot + 1)],
+                        lhsT=qt_of[pair][:, unit, :],
+                        rhs=ctx_of[b][:, unit % H, 0:D],
+                        start=True,
+                        stop=True,
+                    )
+                    product_of[(pair, unit)] = (o_ps[:, D * slot : D * (slot + 1)], guest_d_inv_of[(pair, unit)])
 
         def normalise(bank):
             pair, units = units_of(bank)
@@ -122,15 +145,15 @@ def tile_linearattention_pb_t_kernel(tc, q, k_sum, context, Wp_words, Wp_scales,
             if bank % PAIR_BANKS == 0:
                 om_sb = work.tile([P, PAIR, E], BF16)
                 om_of[pair] = om_sb
-            o_ps, d_inv = product_of[bank]
-            for slot, unit in enumerate(units):
+            for unit in units:
                 h = unit % H
+                product, d_inv = product_of[(pair, unit)]
                 nc.vector.scalar_tensor_tensor(
                     out=om_of[pair][:, unit // H, :].rearrange("p (u m) -> p u m", u=2)[
                         :, :, (D // 2) * h : (D // 2) * (h + 1)
                     ],
-                    in0=o_ps[:, slot, 0:D].rearrange("p (m u) -> p u m", u=2),
-                    scalar=d_inv[:, slot : slot + 1],
+                    in0=product.rearrange("p (m u) -> p u m", u=2),
+                    scalar=d_inv,
                     in1=q_of[b][:, h, a0 + unit // H, :].rearrange("p (m u) -> p u m", u=2),
                     op0=MULT,
                     op1=ADD,

@@ -57,6 +57,10 @@ def tile_linearattention_pb_t_kernel(tc, q, k_sum, context, Wp_words, Wp_scales,
                     if b == 0:
                         nc.sync.dma_start(out=ksum_rows[0 : B * H, :], in_=k_sum.rearrange("b h o d -> (b h o) d"))
                     nc.sync.dma_start(out=ctx_sb[:, :, 0:D], in_=context[b].rearrange("h d e -> d h e"))
+                    if b == 0:
+                        nc.sync.dma_start(
+                            out=w_as_it_comes[:].bitcast(I32), in_=Wp_words[0].rearrange("p n j -> p (n j)").bitcast(I32)
+                        )
                 tiles = slice(width * piece, width * (piece + 1))
                 nc.sync.dma_start(
                     out=q_sb[:, :, tiles, :].rearrange("p h a d -> p h (a d)"),
@@ -67,11 +71,17 @@ def tile_linearattention_pb_t_kernel(tc, q, k_sum, context, Wp_words, Wp_scales,
 
         ksum_rows = const.tile([P, D], BF16)
         nc.vector.memset(ksum_rows[:], 0.0)
+        w_as_it_comes = const.tile([P, PACK * DIM], U8, align_bytes=64)
+        w_codes = const.tile([P, PACK * DIM], U8, align_bytes=64)
         load_batch(0, PAIRS_IN_BATCH)
         load_batch(1, 1)
 
         w_scales = const.tile([P, DIM], U8, align_bytes=64)
         nc.vector.memset(w_scales[:].bitcast(I32), 0)
+        nc.vector.tensor_copy(
+            out=w_codes[:].rearrange("p (n u s) -> p n s u", u=2, s=2),
+            in_=w_as_it_comes[:].rearrange("p (n s u) -> p n s u", u=2, s=2),
+        )
 
         ident_bf16 = const.tile([P, P], BF16)
         make_identity(nc, ident_bf16[:])
@@ -213,7 +223,9 @@ def tile_linearattention_pb_t_kernel(tc, q, k_sum, context, Wp_words, Wp_scales,
                 result = work.tile([P, QUAD, DIM], F32, tag="result_of_vector")
                 nc.vector.tensor_tensor(out=result[:, 0:count, :], in0=out_ps[:, 0:count, :], in1=bias_rows, op=ADD)
             else:
-                result = work.tile([P, QUAD, DIM], F32, tag="result_of_gpsimd")
+                result = (
+                    grouped_of[quad + 1][:].bitcast(F32)[:, 0 : QUAD * DIM].rearrange("p (i n) -> p i n", i=QUAD)
+                )
                 no_bias = work.tile([P, QUAD, DIM], F32)
                 nc.scalar.copy(out=no_bias[:, 0:count, :], in_=out_ps[:, 0:count, :])
                 nc.gpsimd.tensor_tensor(out=result[:, 0:count, :], in0=no_bias[:, 0:count, :], in1=bias_rows, op=ADD)
@@ -226,11 +238,6 @@ def tile_linearattention_pb_t_kernel(tc, q, k_sum, context, Wp_words, Wp_scales,
         def last_of_quad(pair):
             return 0 <= pair < PAIRS and pair % PAIRS_IN_QUAD == PAIRS_IN_QUAD - 1
 
-        w_as_it_comes = const.tile([P, PACK * DIM], U8, align_bytes=64)
-        nc.sync.dma_start(
-            out=w_as_it_comes[:].bitcast(I32), in_=Wp_words[0].rearrange("p n j -> p (n j)").bitcast(I32)
-        )
-        w_codes = const.tile([P, PACK * DIM], U8, align_bytes=64)
         for quadrant in range(4):
             nc.sync.dma_start(
                 out=w_scales[32 * quadrant : 32 * quadrant + 4, :].bitcast(I32),
@@ -269,11 +276,6 @@ def tile_linearattention_pb_t_kernel(tc, q, k_sum, context, Wp_words, Wp_scales,
                 multiply(bank)
                 if bank >= 1:
                     normalise(bank - 1)
-                if step == 2 and part == 0:
-                    nc.vector.tensor_copy(
-                        out=w_codes[:].rearrange("p (n u s) -> p n s u", u=2, s=2),
-                        in_=w_as_it_comes[:].rearrange("p (n s u) -> p n s u", u=2, s=2),
-                    )
                 if part == 0 and step + 2 < PAIRS:
                     transpose_q(step + 2)
                 if part == 1 and step >= 2:

from contextlib import ExitStack

import concourse.mybir as mybir
from concourse.masks import make_identity

BF16 = mybir.dt.bfloat16
F32 = mybir.dt.float32
I32 = mybir.dt.int32
U8 = mybir.dt.uint8
U32 = mybir.dt.uint32
FP8X4 = mybir.dt.float8_e4m3fn_x4
MULT = mybir.AluOpType.mult
ADD = mybir.AluOpType.add

P = 128
B, H, T, D = 16, 4, 1024, 128
E = H * D
DIM = 128
PACK = 4

TILES = T // P
PAIR = 2
PAIR_UNITS = PAIR * H
QUAD = 4
PAIRS = B * TILES // PAIR
PAIRS_IN_BATCH = TILES // PAIR
PAIRS_IN_QUAD = QUAD // PAIR
QUADS = PAIRS // PAIRS_IN_QUAD
BANK_UNITS = 3
PAIR_BANKS = 3
BANK_COLUMNS = 512
CTX_PITCH = 144
AHEAD = 3

FLOPS = 2 * B * H * T * D * D + 2 * B * T * E * DIM


def tile_linearattention_pb_t_kernel(tc, q, k_sum, context, Wp_words, Wp_scales, bp, out):
    nc = tc.nc
    with ExitStack() as stack:
        stack.enter_context(tc.manual_schedule())
        const = stack.enter_context(tc.tile_pool(name="const", bufs=1))
        batch_pool = stack.enter_context(tc.tile_pool(name="batch", bufs=AHEAD + 2))
        work = stack.enter_context(tc.tile_pool(name="work", bufs=4))
        to_vector = stack.enter_context(tc.psum_pool(name="to_vector", bufs=5))
        to_scalar = stack.enter_context(tc.psum_pool(name="to_scalar", bufs=3))

        q_of = {}
        ctx_of = {}

        def load_batch(b, pieces):
            ctx_sb = batch_pool.tile([P, H, CTX_PITCH], BF16)
            q_sb = batch_pool.tile([P, H, TILES, D], BF16)
            width = TILES // pieces
            for piece in range(pieces):
                if piece == min(1, pieces - 1):
                    if b == 0:
                        nc.sync.dma_start(out=ksum_rows[0 : B * H, :], in_=k_sum.rearrange("b h o d -> (b h o) d"))
                    nc.sync.dma_start(out=ctx_sb[:, :, 0:D], in_=context[b].rearrange("h d e -> d h e"))
                    if b == 0:
                        nc.sync.dma_start(
                            out=w_as_it_comes[:].bitcast(I32), in_=Wp_words[0].rearrange("p n j -> p (n j)").bitcast(I32)
                        )
                tiles = slice(width * piece, width * (piece + 1))
                nc.sync.dma_start(
                    out=q_sb[:, :, tiles, :].rearrange("p h a d -> p h (a d)"),
                    in_=q[b].rearrange("h (p a) d -> p h a d", a=TILES)[:, :, tiles, :].rearrange("p h a d -> p h (a d)"),
                )
            ctx_of[b] = ctx_sb
            q_of[b] = q_sb

        ksum_rows = const.tile([P, D], BF16)
        nc.vector.memset(ksum_rows[:], 0.0)
        w_as_it_comes = const.tile([P, PACK * DIM], U8, align_bytes=64)
        w_codes = const.tile([P, PACK * DIM], U8, align_bytes=64)
        load_batch(0, PAIRS_IN_BATCH)
        load_batch(1, 1)

        w_scales = const.tile([P, DIM], U8, align_bytes=64)
        nc.vector.memset(w_scales[:].bitcast(I32), 0)
        nc.vector.tensor_copy(
            out=w_codes[:].rearrange("p (n u s) -> p n s u", u=2, s=2),
            in_=w_as_it_comes[:].rearrange("p (n s u) -> p n s u", u=2, s=2),
        )

        ident_bf16 = const.tile([P, P], BF16)
        make_identity(nc, ident_bf16[:])
        ident_f32 = const.tile([P, P], F32)
        make_identity(nc, ident_f32[:])

        qt_of = {}
        product_of = {}
        guest_d_inv_of = {}
        om_of = {}
        grouped_of = {}
        codes_of = {}
        out_ps_of = {}

        def where(pair):
            return pair // PAIRS_IN_BATCH, PAIR * (pair % PAIRS_IN_BATCH)

        def units_of(bank):
            first = BANK_UNITS * (bank % PAIR_BANKS)
            return bank // PAIR_BANKS, list(range(first, min(first + BANK_UNITS, PAIR_UNITS)))

        def transpose_q(pair):
            b, a0 = where(pair)
            qt_ps = to_scalar.tile([P, PAIR_UNITS, P], BF16, tag="to_scalar")
            for unit in range(PAIR_UNITS):
                nc.tensor.transpose(qt_ps[:, unit, :], q_of[b][:, unit % H, a0 + unit // H, :], ident_bf16[:])
            qt_sb = work.tile([P, PAIR_UNITS, P], BF16)
            nc.scalar.copy(out=qt_sb[:].bitcast(F32), in_=qt_ps[:].bitcast(F32))
            qt_of[pair] = qt_sb

        def multiply(bank):
            pair, units = units_of(bank)
            b, a0 = where(pair)
            o_ps = to_vector.tile([P, BANK_COLUMNS], F32, tag="to_vector")
            if len(units) == BANK_UNITS:
                guest = PAIR_BANKS * (BANK_UNITS - 1) + bank % PAIR_BANKS
                for slot, unit in enumerate(units):
                    nc.tensor.matmul(
                        o_ps[:, 1 + (D + 1) * slot : 1 + (D + 1) * (slot + 1)],
                        lhsT=qt_of[pair][:, unit, :],
                        rhs=ctx_of[b][:, unit % H, 0 : D + 1],
                        start=True,
                        stop=True,
                    )
                nc.tensor.matmul(
                    o_ps[:, 0:1],
                    lhsT=qt_of[pair][:, guest, :],
                    rhs=ctx_of[b][:, guest % H, D : D + 1],
                    start=True,
                    stop=True,
                )
                d_inv = work.tile([P, BANK_UNITS + 1], F32)
                nc.vector.reciprocal(out=d_inv[:], in_=o_ps[:, 0 : (D + 1) * BANK_UNITS + 1 : D + 1])
                for slot, unit in enumerate(units):
                    product_of[(pair, unit)] = (o_ps[:, 1 + (D + 1) * slot : D + 1 + (D + 1) * slot], d_inv[:, slot + 1 : slot + 2])
                guest_d_inv_of[(pair, guest)] = d_inv[:, 0:1]
            else:
                for slot, unit in enumerate(units):
                    nc.tensor.matmul(
                        o_ps[:, D * slot : D * (slot + 1)],
                        lhsT=qt_of[pair][:, unit, :],
                        rhs=ctx_of[b][:, unit % H, 0:D],
                        start=True,
                        stop=True,
                    )
                    product_of[(pair, unit)] = (o_ps[:, D * slot : D * (slot + 1)], guest_d_inv_of[(pair, unit)])

        def normalise(bank):
            pair, units = units_of(bank)
            b, a0 = where(pair)
            if bank % PAIR_BANKS == 0:
                om_sb = work.tile([P, PAIR, E], BF16)
                om_of[pair] = om_sb
            for unit in units:
                h = unit % H
                product, d_inv = product_of[(pair, unit)]
                nc.vector.scalar_tensor_tensor(
                    out=om_of[pair][:, unit // H, :].rearrange("p (u m) -> p u m", u=2)[
                        :, :, (D // 2) * h : (D // 2) * (h + 1)
                    ],
                    in0=product.rearrange("p (m u) -> p u m", u=2),
                    scalar=d_inv,
                    in1=q_of[b][:, h, a0 + unit // H, :].rearrange("p (m u) -> p u m", u=2),
                    op0=MULT,
                    op1=ADD,
                )

        def transpose_om(pair, tiles):
            quad, half = pair // PAIRS_IN_QUAD, pair % PAIRS_IN_QUAD
            if half == 0 and tiles[0] == 0:
                grouped = work.tile([P, QUAD * P * PACK], BF16, align_bytes=64)
                grouped_of[quad] = grouped
            omt_ps = to_scalar.tile([P, PAIR, 2, P], F32, tag="to_scalar")
            for slot, tile_in_pair in enumerate(tiles):
                om_words = om_of[pair][:, tile_in_pair, :].bitcast(F32)
                for u in range(2):
                    nc.tensor.transpose(omt_ps[:, slot, u, :], om_words[:, P * u : P * (u + 1)], ident_f32[:])
            words = P * 2
            first = PAIR * half + tiles[0]
            nc.scalar.copy(
                out=grouped_of[quad][:]
                .bitcast(F32)[:, words * first : words * (first + len(tiles))]
                .rearrange("p (i t u) -> p i t u", i=len(tiles), u=2),
                in_=omt_ps[:, 0 : len(tiles), :, :].rearrange("p i u t -> p i t u"),
            )

        def quantise(quad, first, count):
            if first == 0:
                codes = work.tile([P, QUAD * P], U32, align_bytes=64)
                scales = work.tile([P, QUAD * P], U8, align_bytes=64)
                codes_of[quad] = (codes, scales)
            codes, scales = codes_of[quad]
            tokens = slice(P * first, P * (first + count))
            nc.vector.quantize_mx(
                out=codes[:, tokens].bitcast(FP8X4),
                scales=scales[:, tokens],
                in_=grouped_of[quad][:, PACK * P * first : PACK * P * (first + count)],
            )

        def project(quad, first, count, ring):
            codes, scales = codes_of[quad]
            out_ps = ring.tile([P, QUAD, DIM], F32, tag="to_vector" if ring is to_vector else "to_scalar")
            for i in range(first, first + count):
                nc.tensor.matmul_mx(
                    out=out_ps[:, i - first, :],
                    lhsT=codes[:, P * i : P * (i + 1)].bitcast(FP8X4),
                    lhsT_scale=scales[:, P * i : P * (i + 1)],
                    rhs=w_codes[:].bitcast(FP8X4),
                    rhs_scale=w_scales[:],
                    start=True,
                    stop=True,
                )
            out_ps_of[(quad, first)] = out_ps

        def finish(quad, first, count, on_vector):
            out_ps = out_ps_of[(quad, first)]
            bias_rows = bias[:].unsqueeze(1).to_broadcast([P, count, DIM])
            if on_vector:
                result = work.tile([P, QUAD, DIM], F32, tag="result_of_vector")
                nc.vector.tensor_tensor(out=result[:, 0:count, :], in0=out_ps[:, 0:count, :], in1=bias_rows, op=ADD)
            else:
                result = (
                    grouped_of[quad + 1][:].bitcast(F32)[:, 0 : QUAD * DIM].rearrange("p (i n) -> p i n", i=QUAD)
                )
                no_bias = work.tile([P, QUAD, DIM], F32)
                nc.scalar.copy(out=no_bias[:, 0:count, :], in_=out_ps[:, 0:count, :])
                nc.gpsimd.tensor_tensor(out=result[:, 0:count, :], in0=no_bias[:, 0:count, :], in1=bias_rows, op=ADD)
            b, a0 = where(quad * PAIRS_IN_QUAD)
            nc.sync.dma_start(
                out=out[b].rearrange("(p a) n -> p a n", a=TILES)[:, a0 + first : a0 + first + count, :],
                in_=result[:, 0:count, :],
            )

        def last_of_quad(pair):
            return 0 <= pair < PAIRS and pair % PAIRS_IN_QUAD == PAIRS_IN_QUAD - 1

        for quadrant in range(4):
            nc.sync.dma_start(
                out=w_scales[32 * quadrant : 32 * quadrant + 4, :].bitcast(I32),
                in_=Wp_scales[0, 4 * quadrant : 4 * quadrant + 4, :].bitcast(I32),
            )

        bias_bf16 = const.tile([P, DIM], BF16)
        nc.sync.dma_start(out=bias_bf16[:], in_=bp.partition_broadcast(P))

        for b in range(2, AHEAD):
            load_batch(b, 1)

        transpose_q(0)

        ksum_ps = to_scalar.tile([P, PAIR_UNITS, P], BF16, tag="to_scalar")
        nc.tensor.transpose(ksum_ps[:, 0, :], ksum_rows[:], ident_bf16[:])
        ksum_cols = const.tile([P, B * H], BF16)
        nc.scalar.copy(out=ksum_cols[:], in_=ksum_ps[:, 0, 0 : B * H])

        def add_k_sum(b):
            nc.gpsimd.tensor_copy(
                out=ctx_of[b][:, :, D : D + 1], in_=ksum_cols[:, H * b : H * (b + 1)].unsqueeze(2)
            )

        for b in range(AHEAD):
            add_k_sum(b)
        bias = const.tile([P, DIM], F32)
        nc.gpsimd.tensor_copy(out=bias[:], in_=bias_bf16[:])
        transpose_q(1)
        for step in range(PAIRS):
            if step % PAIRS_IN_BATCH == 0 and step // PAIRS_IN_BATCH + AHEAD < B:
                load_batch(step // PAIRS_IN_BATCH + AHEAD, 1)
                add_k_sum(step // PAIRS_IN_BATCH + AHEAD)
            for part in range(PAIR_BANKS):
                bank = PAIR_BANKS * step + part
                multiply(bank)
                if bank >= 1:
                    normalise(bank - 1)
                if part == 0 and step + 2 < PAIRS:
                    transpose_q(step + 2)
                if part == 1 and step >= 2:
                    transpose_om(step - 2, [0, 1])
                if part == 2 and last_of_quad(step - 3):
                    quantise((step - 3) // PAIRS_IN_QUAD, 0, QUAD)
                if part == 2 and last_of_quad(step - 5):
                    project((step - 5) // PAIRS_IN_QUAD, 0, QUAD, to_scalar)
                    finish((step - 5) // PAIRS_IN_QUAD, 0, QUAD, False)

        last = QUADS - 1
        normalise(PAIR_BANKS * PAIRS - 1)
        transpose_om(PAIRS - 2, [0, 1])
        transpose_om(PAIRS - 1, [0])
        project(last - 2, 0, QUAD, to_scalar)
        transpose_om(PAIRS - 1, [1])
        quantise(last - 1, 0, QUAD)
        project(last - 1, 0, QUAD, to_vector)
        pieces = [(0, PAIR), (PAIR, 1), (PAIR + 1, 1)]
        for first, count in pieces:
            quantise(last, first, count)
            project(last, first, count, to_vector)
        finish(last - 2, 0, QUAD, False)
        finish(last - 1, 0, QUAD, True)
        for first, count in pieces:
            finish(last, first, count, True)
